import numpy as np
import ml_dtypes


def mxq(x, axis, fmt="e4m3"):
    dtype, down = {"e4m3": (ml_dtypes.float8_e4m3fn, 7), "e5m2": (ml_dtypes.float8_e5m2, 14)}[fmt]
    v = np.moveaxis(np.asarray(x, np.float32).astype(ml_dtypes.bfloat16).astype(np.float64), axis, -1)
    blocks = v.reshape(v.shape[:-1] + (-1, 32))
    amax = np.abs(blocks).max(-1, keepdims=True)
    byte = np.maximum(np.where(amax > 0, np.frexp(amax)[1] - 1 + 127, 0) - down, 1)
    scale = np.exp2(byte - 127.0)
    codes = (blocks / scale).astype(np.float32).astype(dtype).astype(np.float64)
    return np.moveaxis((codes * scale).reshape(v.shape), -1, axis)


WIDE = False


def mx_kscale(k):
    if not WIDE:
        return np.ones(k)
    levels = np.array([10, -10, 5, -5, 0])
    a = np.random.permutation(np.resize(levels, k // 512 * 4)).reshape(k // 512, 4)
    idx = np.arange(k)
    return np.exp2(a[idx // 512, idx % 128 // 32])


BF16 = ml_dtypes.bfloat16


def bf(x):
    return np.asarray(x, np.float32).astype(BF16)


def f64(x):
    return np.asarray(x).astype(np.float64)


HI, WS, D, F, NH = 32, 4, 512, 2048, 8
EPS = 1e-5
N = HI * HI
NWS = HI // WS
NW = NWS * NWS
NPW = WS * WS
HD = D // NH
SH = WS // 2


def layer_norm(x, g, b):
    m = x.mean(-1, keepdims=True)
    v = ((x - m) ** 2).mean(-1, keepdims=True)
    return (x - m) / np.sqrt(v + EPS) * g + b


def win_part(img):
    return img.reshape(NWS, WS, NWS, WS, D).swapaxes(1, 2).reshape(NW, NPW, D)


def win_merge(win):
    return win.reshape(NWS, NWS, WS, WS, D).swapaxes(1, 2).reshape(HI, HI, D)


def heads(t):
    return np.ascontiguousarray(t.reshape(NW, NPW, NH, HD).swapaxes(1, 2))


def setup_inputs():
    s = mx_kscale(D)
    return {"x_win": bf(np.random.standard_normal((N, D)) * 1.5),
            "ln3_g": bf((1.0 + 0.1 * np.random.standard_normal(D)) * s),
            "ln3_b": bf(0.1 * np.random.standard_normal(D) * s),
            "qkv2_w": bf(np.random.standard_normal((D, 3 * D)) / np.sqrt(D) / s[:, None]),
            "qkv2_b": bf(0.1 * np.random.standard_normal(3 * D))}


def reference(x_win, ln3_g, ln3_b, qkv2_w, qkv2_b):
    h = layer_norm(f64(x_win), f64(ln3_g), f64(ln3_b))
    img = win_merge(h.reshape(NW, NPW, D))
    shifted = win_part(np.roll(img, (-SH, -SH), (0, 1))).reshape(N, D)
    qkv = (mxq(shifted, 1, "e4m3") @ mxq(f64(qkv2_w), 0, "e4m3")) + f64(qkv2_b)
    q, k, v = np.split(qkv, 3, axis=-1)
    return heads(q), heads(k), heads(v)

@@ -1,0 +1,242 @@
+from contextlib import ExitStack
+
+import concourse.mybir as mybir
+from concourse.masks import make_identity
+
+F32 = mybir.dt.float32
+BF16 = mybir.dt.bfloat16
+I32 = mybir.dt.int32
+U32 = mybir.dt.uint32
+U8 = mybir.dt.uint8
+FP8X4 = mybir.dt.float8_e4m3fn_x4
+ACT = mybir.ActivationFunctionType
+ALU = mybir.AluOpType
+
+P = 128
+PACK = 4
+D = P * PACK
+GRID = 8
+WINDOWS = GRID * GRID
+LANES = 8
+ROW_LANES = 4
+ROUNDS = LANES // ROW_LANES
+PARTS = 3
+HEADS = 8
+HEAD_DIM = D // HEADS
+STORE_HEADS = 4
+EPS = 1e-5
+
+FLOPS = 2 * (P * LANES) * D * (PARTS * D)
+
+
+def tile_swintransformerblock_pa_kernel(
+    tc, x_win, ln3_g, ln3_b, qkv2_w, qkv2_b, out_0, out_1, out_2
+):
+    nc = tc.nc
+    outs = (out_0, out_1, out_2)
+
+    with ExitStack() as ctx:
+        const = ctx.enter_context(tc.tile_pool(name="const", bufs=1))
+        keep = ctx.enter_context(tc.tile_pool(name="keep", bufs=1))
+        small = ctx.enter_context(tc.tile_pool(name="small", bufs=2))
+        z_pool = ctx.enter_context(tc.tile_pool(name="z_pool", bufs=4))
+        stage = ctx.enter_context(tc.tile_pool(name="stage", bufs=2))
+        t_psum = ctx.enter_context(tc.psum_pool(name="t_psum", bufs=1))
+        acc_psum = ctx.enter_context(tc.psum_pool(name="acc_psum", bufs=4))
+
+        x_sb = keep.tile([P, LANES, D], BF16)
+        x_rows = x_win.rearrange("(i j) d -> i j d", j=LANES)
+        w_sb = keep.tile([P, PARTS, PACK, D], BF16)
+        w_rows = qkv2_w.rearrange("(t p) (s n) -> p s t n", p=P, s=PARTS)
+        nc.sync.dma_start(out=x_sb[:, 0:ROW_LANES, :], in_=x_rows[:, 0:ROW_LANES, :])
+        nc.sync.dma_start(out=w_sb[:, 0, :, :], in_=w_rows[:, 0, :, :])
+        nc.sync.dma_start(out=x_sb[:, ROW_LANES:LANES, :], in_=x_rows[:, ROW_LANES:LANES, :])
+        nc.sync.dma_start(out=w_sb[:, 1, :, :], in_=w_rows[:, 1, :, :])
+        nc.sync.dma_start(out=w_sb[:, 2, :, :], in_=w_rows[:, 2, :, :])
+
+        gain_rows = const.tile([P, P], BF16)
+        nc.vector.memset(gain_rows[:].bitcast(I32), 0)
+        nc.scalar.dma_start(out=gain_rows[0:PACK, :], in_=ln3_g.rearrange("(t p) -> t p", p=P))
+        nc.scalar.dma_start(
+            out=gain_rows[PACK : 2 * PACK, :], in_=ln3_b.rearrange("(t p) -> t p", p=P)
+        )
+        bias_row = const.tile([P, PARTS * D], BF16)
+        nc.vector.memset(bias_row[:].bitcast(I32), 0)
+        nc.scalar.dma_start(out=bias_row[0:1, :], in_=qkv2_b.rearrange("(o n) -> o n", o=1))
+
+        eps = const.tile([P, 1], F32)
+        nc.vector.memset(eps[:], EPS)
+        table_warmer = const.tile([P, 1], F32)
+        nc.scalar.activation(out=table_warmer[:], in_=eps[:], func=ACT.Sqrt)
+
+        ident = const.tile([P, P], F32)
+        make_identity(nc, ident[:])
+
+        take_below = const.tile([P, P], F32)
+        from_half = ident[:].rearrange("i (w h) -> i w h", h=2)
+        to_half = take_below[:].rearrange("i (w h) -> i w h", h=2)
+        nc.vector.tensor_copy(out=to_half[:, :, 0], in_=from_half[:, :, 1])
+        nc.vector.tensor_copy(
+            out=to_half[:, 0 : WINDOWS - GRID, 1], in_=from_half[:, GRID:WINDOWS, 0]
+        )
+        nc.vector.tensor_copy(
+            out=to_half[:, WINDOWS - GRID : WINDOWS, 1], in_=from_half[:, 0:GRID, 0]
+        )
+        take_below_right = const.tile([P, P], F32)
+        from_row = take_below[:].rearrange("i (r e) -> i r e", e=2 * GRID)
+        to_row = take_below_right[:].rearrange("i (r e) -> i r e", e=2 * GRID)
+        nc.vector.tensor_copy(out=to_row[:, :, 0 : 2 * GRID - 2], in_=from_row[:, :, 2 : 2 * GRID])
+        nc.vector.tensor_copy(out=to_row[:, :, 2 * GRID - 2 : 2 * GRID], in_=from_row[:, :, 0:2])
+
+        gain_rows_f32 = const.tile([P, P], F32)
+        nc.vector.tensor_copy(out=gain_rows_f32[:], in_=gain_rows[:])
+        gain_bank = acc_psum.tile([P, D], F32, tag="acc")
+        nc.tensor.transpose(out=gain_bank[:, 0:P], in_=gain_rows_f32[:], identity=ident[:])
+        gain_cols = const.tile([P, 2 * PACK], F32)
+        nc.vector.tensor_copy(out=gain_cols[:], in_=gain_bank[:, 0 : 2 * PACK])
+
+        ones = const.tile([P, P], BF16)
+        nc.vector.memset(ones[:], 1.0)
+        bias_all = const.tile([P, PARTS, D], F32)
+        for s in range(PARTS):
+            bias_bank = acc_psum.tile([P, D], F32, tag="acc")
+            nc.tensor.matmul(
+                out=bias_bank[:],
+                lhsT=ones[:],
+                rhs=bias_row[:, s * D : (s + 1) * D],
+                start=True,
+                stop=True,
+            )
+            nc.scalar.copy(out=bias_all[:, s, :], in_=bias_bank[:])
+
+        s_codes = keep.tile([P, ROUNDS, ROW_LANES * P], U32, align_bytes=64)
+        s_scales = keep.tile([P, ROUNDS, ROW_LANES * P], U8, align_bytes=64)
+        w_codes = keep.tile([P, PARTS, D], U32, align_bytes=64)
+        w_scales = keep.tile([P, PARTS, D], U8, align_bytes=64)
+        out_sb = keep.tile([P, PARTS, HEADS, LANES, HEAD_DIM], F32)
+
+        def regroup(copy, grouped, planes):
+            copy(
+                out=grouped[:].rearrange("p (c i) t -> p c t i", i=4),
+                in_=planes.rearrange("p t (c i) -> p c t i", i=4),
+            )
+
+        def quantise_weights(s, copy):
+            w_grouped = stage.tile([P, D, PACK], BF16, align_bytes=64)
+            regroup(copy, w_grouped, w_sb[:, s, :, :])
+            nc.vector.quantize_mx(
+                out=w_codes[:, s, :].bitcast(FP8X4),
+                scales=w_scales[:, s, :],
+                in_=w_grouped[:].rearrange("p c t -> p (c t)"),
+            )
+
+        def row_statistics(r):
+            stats = small.tile([P, ROW_LANES, 6], F32)
+            mean_var = small.tile([P, ROW_LANES, 2], F32)
+            for u in range(ROW_LANES):
+                nc.vector.bn_stats(out=stats[:, u, :], in_=x_sb[:, r * ROW_LANES + u, :])
+            for u in range(ROW_LANES):
+                nc.vector.bn_aggr(out=mean_var[:, u, :], in_=stats[:, u, :])
+            std = small.tile([P, ROW_LANES], F32)
+            nc.scalar.activation(out=std[:], in_=mean_var[:, :, 1], func=ACT.Sqrt, bias=eps[:])
+            rstd = small.tile([P, ROW_LANES], F32)
+            nc.vector.reciprocal(out=rstd[:], in_=std[:])
+            shift = small.tile([P, ROW_LANES], F32)
+            nc.vector.scalar_tensor_tensor(
+                out=shift[:],
+                in0=mean_var[:, :, 0],
+                scalar=-1.0,
+                in1=rstd[:],
+                op0=ALU.mult,
+                op1=ALU.mult,
+            )
+            return rstd, shift
+
+        def normalise_and_transpose(r, rstd, shift):
+            z_banks = [
+                t_psum.tile([P, ROW_LANES, P], F32, name="z_bank%d" % t, tag="z_bank%d" % t)
+                for t in range(PACK)
+            ]
+            for u in range(ROW_LANES):
+                z = z_pool.tile([P, D], F32)
+                nc.scalar.activation(
+                    out=z[:],
+                    in_=x_sb[:, r * ROW_LANES + u, :],
+                    func=ACT.Identity,
+                    scale=rstd[:, u : u + 1],
+                    bias=shift[:, u : u + 1],
+                )
+                q = (u + 2) % ROW_LANES
+                permutation = take_below_right if u < 2 else take_below
+                for t in range(PACK):
+                    nc.tensor.transpose(
+                        out=z_banks[t][:, q, :],
+                        in_=z[:, t * P : (t + 1) * P],
+                        identity=permutation[:],
+                    )
+            return z_banks
+
+        def scale_and_quantise(r, z_banks):
+            h_planes = stage.tile([P, PACK, ROW_LANES * P], BF16)
+            for t in range(PACK):
+                nc.scalar.activation(
+                    out=h_planes[:, t, :],
+                    in_=z_banks[t][:].rearrange("p q m -> p (q m)"),
+                    func=ACT.Identity,
+                    scale=gain_cols[:, t : t + 1],
+                    bias=gain_cols[:, PACK + t : PACK + t + 1],
+                )
+            h_grouped = stage.tile([P, ROW_LANES * P, PACK], BF16, align_bytes=64)
+            regroup(nc.vector.tensor_copy, h_grouped, h_planes[:])
+            nc.vector.quantize_mx(
+                out=s_codes[:, r, :].bitcast(FP8X4),
+                scales=s_scales[:, r, :],
+                in_=h_grouped[:].rearrange("p c t -> p (c t)"),
+            )
+
+        def project(r, s):
+            for q in range(ROW_LANES):
+                acc = acc_psum.tile([P, D], F32, tag="acc")
+                nc.tensor.matmul_mx(
+                    out=acc[:],
+                    lhsT=s_codes[:, r, q * P : (q + 1) * P].bitcast(FP8X4),
+                    lhsT_scale=s_scales[:, r, q * P : (q + 1) * P],
+                    rhs=w_codes[:, s, :].bitcast(FP8X4),
+                    rhs_scale=w_scales[:, s, :],
+                    start=True,
+                    stop=True,
+                )
+                nc.vector.tensor_tensor(
+                    out=out_sb[:, s, :, r * ROW_LANES + q, :],
+                    in0=acc[:].rearrange("m (n c) -> m n c", c=HEAD_DIM),
+                    in1=bias_all[:, s, :].rearrange("m (n c) -> m n c", c=HEAD_DIM),
+                    op=ALU.add,
+                )
+            dram = outs[s].rearrange("w n (h r q) c -> h r w n (q c)", h=2, r=ROUNDS)
+            for half in range(2):
+                for n0 in range(0, HEADS, STORE_HEADS):
+                    nc.sync.dma_start(
+                        out=dram[half, r, :, n0 : n0 + STORE_HEADS, :],
+                        in_=out_sb[
+                            half:P:2,
+                            s,
+                            n0 : n0 + STORE_HEADS,
+                            r * ROW_LANES : (r + 1) * ROW_LANES,
+                            :,
+                        ].rearrange("m n q c -> m n (q c)"),
+                    )
+
+        rstd0, shift0 = row_statistics(0)
+        z_banks0 = normalise_and_transpose(0, rstd0, shift0)
+        quantise_weights(0, nc.vector.tensor_copy)
+        rstd1, shift1 = row_statistics(1)
+        scale_and_quantise(0, z_banks0)
+        project(0, 0)
+        z_banks1 = normalise_and_transpose(1, rstd1, shift1)
+        quantise_weights(1, nc.scalar.copy)
+        project(0, 1)
+        quantise_weights(2, nc.scalar.copy)
+        project(0, 2)
+        scale_and_quantise(1, z_banks1)
+        for s in range(PARTS):
+            project(1, s)

@@ -23,7 +23,10 @@ ROUNDS = LANES // ROW_LANES
 PARTS = 3
 HEADS = 8
 HEAD_DIM = D // HEADS
-STORE_HEADS = 4
+PASS_HEADS = 4
+PASS_COLS = PASS_HEADS * HEAD_DIM
+BANK_LANES = 2
+LOAD_LANES = 2
 EPS = 1e-5
 
 FLOPS = 2 * (P * LANES) * D * (PARTS * D)
@@ -36,6 +39,7 @@ def tile_swintransformerblock_pa_kernel(
     outs = (out_0, out_1, out_2)
 
     with ExitStack() as ctx:
+        ctx.enter_context(tc.manual_schedule())
         const = ctx.enter_context(tc.tile_pool(name="const", bufs=1))
         keep = ctx.enter_context(tc.tile_pool(name="keep", bufs=1))
         small = ctx.enter_context(tc.tile_pool(name="small", bufs=2))
@@ -48,21 +52,31 @@ def tile_swintransformerblock_pa_kernel(
         x_rows = x_win.rearrange("(i j) d -> i j d", j=LANES)
         w_sb = keep.tile([P, PARTS, PACK, D], BF16)
         w_rows = qkv2_w.rearrange("(t p) (s n) -> p s t n", p=P, s=PARTS)
-        nc.sync.dma_start(out=x_sb[:, 0:ROW_LANES, :], in_=x_rows[:, 0:ROW_LANES, :])
-        nc.sync.dma_start(out=w_sb[:, 0, :, :], in_=w_rows[:, 0, :, :])
-        nc.sync.dma_start(out=x_sb[:, ROW_LANES:LANES, :], in_=x_rows[:, ROW_LANES:LANES, :])
-        nc.sync.dma_start(out=w_sb[:, 1, :, :], in_=w_rows[:, 1, :, :])
-        nc.sync.dma_start(out=w_sb[:, 2, :, :], in_=w_rows[:, 2, :, :])
-
         gain_rows = const.tile([P, P], BF16)
         nc.vector.memset(gain_rows[:].bitcast(I32), 0)
-        nc.scalar.dma_start(out=gain_rows[0:PACK, :], in_=ln3_g.rearrange("(t p) -> t p", p=P))
-        nc.scalar.dma_start(
+        bias_all = const.tile([P, PARTS, D], BF16)
+
+        def load_x(lane0):
+            lanes = slice(lane0, lane0 + LOAD_LANES)
+            nc.sync.dma_start(out=x_sb[:, lanes, :], in_=x_rows[:, lanes, :])
+
+        def load_w(s):
+            nc.sync.dma_start(out=w_sb[:, s, :, :], in_=w_rows[:, s, :, :])
+
+        load_x(0)
+        load_x(LOAD_LANES)
+        nc.sync.dma_start(out=gain_rows[0:PACK, :], in_=ln3_g.rearrange("(t p) -> t p", p=P))
+        nc.sync.dma_start(
             out=gain_rows[PACK : 2 * PACK, :], in_=ln3_b.rearrange("(t p) -> t p", p=P)
         )
-        bias_row = const.tile([P, PARTS * D], BF16)
-        nc.vector.memset(bias_row[:].bitcast(I32), 0)
-        nc.scalar.dma_start(out=bias_row[0:1, :], in_=qkv2_b.rearrange("(o n) -> o n", o=1))
+        load_w(0)
+        load_x(2 * LOAD_LANES)
+        load_x(3 * LOAD_LANES)
+        nc.sync.dma_start(
+            out=bias_all[:].rearrange("m s n -> m (s n)"), in_=qkv2_b.partition_broadcast(P)
+        )
+        load_w(1)
+        load_w(2)
 
         eps = const.tile([P, 1], F32)
         nc.vector.memset(eps[:], EPS)
@@ -88,55 +102,46 @@ def tile_swintransformerblock_pa_kernel(
         nc.vector.tensor_copy(out=to_row[:, :, 0 : 2 * GRID - 2], in_=from_row[:, :, 2 : 2 * GRID])
         nc.vector.tensor_copy(out=to_row[:, :, 2 * GRID - 2 : 2 * GRID], in_=from_row[:, :, 0:2])
 
-        gain_rows_f32 = const.tile([P, P], F32)
-        nc.vector.tensor_copy(out=gain_rows_f32[:], in_=gain_rows[:])
-        gain_bank = acc_psum.tile([P, D], F32, tag="acc")
-        nc.tensor.transpose(out=gain_bank[:, 0:P], in_=gain_rows_f32[:], identity=ident[:])
-        gain_cols = const.tile([P, 2 * PACK], F32)
-        nc.vector.tensor_copy(out=gain_cols[:], in_=gain_bank[:, 0 : 2 * PACK])
-
-        ones = const.tile([P, P], BF16)
-        nc.vector.memset(ones[:], 1.0)
-        bias_all = const.tile([P, PARTS, D], F32)
-        for s in range(PARTS):
-            bias_bank = acc_psum.tile([P, D], F32, tag="acc")
-            nc.tensor.matmul(
-                out=bias_bank[:],
-                lhsT=ones[:],
-                rhs=bias_row[:, s * D : (s + 1) * D],
-                start=True,
-                stop=True,
-            )
-            nc.scalar.copy(out=bias_all[:, s, :], in_=bias_bank[:])
-
         s_codes = keep.tile([P, ROUNDS, ROW_LANES * P], U32, align_bytes=64)
         s_scales = keep.tile([P, ROUNDS, ROW_LANES * P], U8, align_bytes=64)
         w_codes = keep.tile([P, PARTS, D], U32, align_bytes=64)
         w_scales = keep.tile([P, PARTS, D], U8, align_bytes=64)
         out_sb = keep.tile([P, PARTS, HEADS, LANES, HEAD_DIM], F32)
 
-        def regroup(copy, grouped, planes):
+        gain_cols = const.tile([P, 2 * PACK], F32)
+
+        def gains_onto_partitions():
+            gain_rows_f32 = const.tile([P, P], F32)
+            nc.vector.tensor_copy(out=gain_rows_f32[:], in_=gain_rows[:])
+            gain_bank = acc_psum.tile([P, P], F32, tag="acc")
+            nc.tensor.transpose(out=gain_bank[:], in_=gain_rows_f32[:], identity=ident[:])
+            nc.scalar.copy(out=gain_cols[:], in_=gain_bank[:, 0 : 2 * PACK])
+
+        def regroup(copy, planes, name):
+            grouped = stage.tile([P, D, PACK], BF16, align_bytes=64, name=name, tag=name)
             copy(
                 out=grouped[:].rearrange("p (c i) t -> p c t i", i=4),
                 in_=planes.rearrange("p t (c i) -> p c t i", i=4),
             )
+            return grouped
 
-        def quantise_weights(s, copy):
-            w_grouped = stage.tile([P, D, PACK], BF16, align_bytes=64)
-            regroup(copy, w_grouped, w_sb[:, s, :, :])
+        def quantise(grouped, codes, scales):
             nc.vector.quantize_mx(
-                out=w_codes[:, s, :].bitcast(FP8X4),
-                scales=w_scales[:, s, :],
-                in_=w_grouped[:].rearrange("p c t -> p (c t)"),
+                out=codes.bitcast(FP8X4),
+                scales=scales,
+                in_=grouped[:].rearrange("p c t -> p (c t)"),
             )
 
-        def row_statistics(r):
+        def row_moments(r):
             stats = small.tile([P, ROW_LANES, 6], F32)
             mean_var = small.tile([P, ROW_LANES, 2], F32)
             for u in range(ROW_LANES):
                 nc.vector.bn_stats(out=stats[:, u, :], in_=x_sb[:, r * ROW_LANES + u, :])
             for u in range(ROW_LANES):
                 nc.vector.bn_aggr(out=mean_var[:, u, :], in_=stats[:, u, :])
+            return mean_var
+
+        def row_scales(mean_var):
             std = small.tile([P, ROW_LANES], F32)
             nc.scalar.activation(out=std[:], in_=mean_var[:, :, 1], func=ACT.Sqrt, bias=eps[:])
             rstd = small.tile([P, ROW_LANES], F32)
@@ -176,67 +181,87 @@ def tile_swintransformerblock_pa_kernel(
                     )
             return z_banks
 
-        def scale_and_quantise(r, z_banks):
+        def gain_out_of_psum(z_banks, vector_banks):
             h_planes = stage.tile([P, PACK, ROW_LANES * P], BF16)
             for t in range(PACK):
-                nc.scalar.activation(
-                    out=h_planes[:, t, :],
-                    in_=z_banks[t][:].rearrange("p q m -> p (q m)"),
-                    func=ACT.Identity,
-                    scale=gain_cols[:, t : t + 1],
-                    bias=gain_cols[:, PACK + t : PACK + t + 1],
-                )
-            h_grouped = stage.tile([P, ROW_LANES * P, PACK], BF16, align_bytes=64)
-            regroup(nc.vector.tensor_copy, h_grouped, h_planes[:])
-            nc.vector.quantize_mx(
-                out=s_codes[:, r, :].bitcast(FP8X4),
-                scales=s_scales[:, r, :],
-                in_=h_grouped[:].rearrange("p c t -> p (c t)"),
-            )
+                z_bank = z_banks[t][:].rearrange("p q m -> p (q m)")
+                gain = gain_cols[:, t : t + 1]
+                bias = gain_cols[:, PACK + t : PACK + t + 1]
+                if t < PACK - vector_banks:
+                    nc.scalar.activation(
+                        out=h_planes[:, t, :], in_=z_bank, func=ACT.Identity, scale=gain, bias=bias
+                    )
+                else:
+                    nc.vector.tensor_scalar(
+                        out=h_planes[:, t, :],
+                        in0=z_bank,
+                        scalar1=gain,
+                        scalar2=bias,
+                        op0=ALU.mult,
+                        op1=ALU.add,
+                    )
+            return h_planes
 
         def project(r, s):
-            for q in range(ROW_LANES):
-                acc = acc_psum.tile([P, D], F32, tag="acc")
-                nc.tensor.matmul_mx(
-                    out=acc[:],
-                    lhsT=s_codes[:, r, q * P : (q + 1) * P].bitcast(FP8X4),
-                    lhsT_scale=s_scales[:, r, q * P : (q + 1) * P],
-                    rhs=w_codes[:, s, :].bitcast(FP8X4),
-                    rhs_scale=w_scales[:, s, :],
-                    start=True,
-                    stop=True,
-                )
-                nc.vector.tensor_tensor(
-                    out=out_sb[:, s, :, r * ROW_LANES + q, :],
-                    in0=acc[:].rearrange("m (n c) -> m n c", c=HEAD_DIM),
-                    in1=bias_all[:, s, :].rearrange("m (n c) -> m n c", c=HEAD_DIM),
-                    op=ALU.add,
-                )
             dram = outs[s].rearrange("w n (h r q) c -> h r w n (q c)", h=2, r=ROUNDS)
-            for half in range(2):
-                for n0 in range(0, HEADS, STORE_HEADS):
+            for n0 in range(0, HEADS, PASS_HEADS):
+                cols = slice(n0 * HEAD_DIM, n0 * HEAD_DIM + PASS_COLS)
+                for q0 in range(0, ROW_LANES, BANK_LANES):
+                    acc = acc_psum.tile([P, BANK_LANES, PASS_COLS], F32, tag="acc")
+                    for e in range(BANK_LANES):
+                        rows = slice((q0 + e) * P, (q0 + e + 1) * P)
+                        nc.tensor.matmul_mx(
+                            out=acc[:, e, :],
+                            lhsT=s_codes[:, r, rows].bitcast(FP8X4),
+                            lhsT_scale=s_scales[:, r, rows],
+                            rhs=w_codes[:, s, cols].bitcast(FP8X4),
+                            rhs_scale=w_scales[:, s, cols],
+                            start=True,
+                            stop=True,
+                        )
+                    lane0 = r * ROW_LANES + q0
+                    nc.vector.tensor_tensor(
+                        out=out_sb[
+                            :, s, n0 : n0 + PASS_HEADS, lane0 : lane0 + BANK_LANES, :
+                        ].rearrange("m n q c -> m q n c"),
+                        in0=acc[:].rearrange("m q (n c) -> m q n c", c=HEAD_DIM),
+                        in1=bias_all[:, s, cols]
+                        .rearrange("m (o n c) -> m o n c", o=1, c=HEAD_DIM)
+                        .to_broadcast([P, BANK_LANES, PASS_HEADS, HEAD_DIM]),
+                        op=ALU.add,
+                    )
+                for half in range(2):
                     nc.sync.dma_start(
-                        out=dram[half, r, :, n0 : n0 + STORE_HEADS, :],
+                        out=dram[half, r, :, n0 : n0 + PASS_HEADS, :],
                         in_=out_sb[
                             half:P:2,
                             s,
-                            n0 : n0 + STORE_HEADS,
+                            n0 : n0 + PASS_HEADS,
                             r * ROW_LANES : (r + 1) * ROW_LANES,
                             :,
                         ].rearrange("m n q c -> m n (q c)"),
                     )
 
-        rstd0, shift0 = row_statistics(0)
+        rstd0, shift0 = row_scales(row_moments(0))
         z_banks0 = normalise_and_transpose(0, rstd0, shift0)
-        quantise_weights(0, nc.vector.tensor_copy)
-        rstd1, shift1 = row_statistics(1)
-        scale_and_quantise(0, z_banks0)
+        gains_onto_partitions()
+        w_grouped0 = regroup(nc.vector.tensor_copy, w_sb[:, 0, :, :], "w_grouped")
+        mean_var1 = row_moments(1)
+        quantise(w_grouped0, w_codes[:, 0, :], w_scales[:, 0, :])
+        h_planes0 = gain_out_of_psum(z_banks0, vector_banks=2)
+        h_grouped0 = regroup(nc.vector.tensor_copy, h_planes0[:], "h_grouped")
+        rstd1, shift1 = row_scales(mean_var1)
+        quantise(h_grouped0, s_codes[:, 0, :], s_scales[:, 0, :])
+        w_grouped1 = regroup(nc.scalar.copy, w_sb[:, 1, :, :], "w_grouped")
         project(0, 0)
+        quantise(w_grouped1, w_codes[:, 1, :], w_scales[:, 1, :])
         z_banks1 = normalise_and_transpose(1, rstd1, shift1)
-        quantise_weights(1, nc.scalar.copy)
+        w_grouped2 = regroup(nc.scalar.copy, w_sb[:, 2, :, :], "w_grouped")
         project(0, 1)
-        quantise_weights(2, nc.scalar.copy)
+        quantise(w_grouped2, w_codes[:, 2, :], w_scales[:, 2, :])
+        h_planes1 = gain_out_of_psum(z_banks1, vector_banks=0)
         project(0, 2)
-        scale_and_quantise(1, z_banks1)
+        h_grouped1 = regroup(nc.vector.tensor_copy, h_planes1[:], "h_grouped")
+        quantise(h_grouped1, s_codes[:, 1, :], s_scales[:, 1, :])
         for s in range(PARTS):
             project(1, s)

@@ -164,13 +164,23 @@ def tile_swintransformerblock_pa_kernel(
             ]
             for u in range(ROW_LANES):
                 z = z_pool.tile([P, D], F32)
-                nc.scalar.activation(
-                    out=z[:],
-                    in_=x_sb[:, r * ROW_LANES + u, :],
-                    func=ACT.Identity,
-                    scale=rstd[:, u : u + 1],
-                    bias=shift[:, u : u + 1],
-                )
+                if u < ROW_LANES // 2:
+                    nc.scalar.activation(
+                        out=z[:],
+                        in_=x_sb[:, r * ROW_LANES + u, :],
+                        func=ACT.Identity,
+                        scale=rstd[:, u : u + 1],
+                        bias=shift[:, u : u + 1],
+                    )
+                else:
+                    nc.gpsimd.tensor_scalar(
+                        out=z[:],
+                        in0=x_sb[:, r * ROW_LANES + u, :],
+                        scalar1=rstd[:, u : u + 1],
+                        scalar2=shift[:, u : u + 1],
+                        op0=ALU.mult,
+                        op1=ALU.add,
+                    )
                 q = (u + 2) % ROW_LANES
                 permutation = take_below_right if u < 2 else take_below
                 for t in range(PACK):
@@ -245,8 +255,8 @@ def tile_swintransformerblock_pa_kernel(
         rstd0, shift0 = row_scales(row_moments(0))
         z_banks0 = normalise_and_transpose(0, rstd0, shift0)
         gains_onto_partitions()
-        w_grouped0 = regroup(nc.vector.tensor_copy, w_sb[:, 0, :, :], "w_grouped")
         mean_var1 = row_moments(1)
+        w_grouped0 = regroup(nc.vector.tensor_copy, w_sb[:, 0, :, :], "w_grouped")
         quantise(w_grouped0, w_codes[:, 0, :], w_scales[:, 0, :])
         h_planes0 = gain_out_of_psum(z_banks0, vector_banks=2)
         h_grouped0 = regroup(nc.vector.tensor_copy, h_planes0[:], "h_grouped")
@@ -260,8 +270,8 @@ def tile_swintransformerblock_pa_kernel(
         project(0, 1)
         quantise(w_grouped2, w_codes[:, 2, :], w_scales[:, 2, :])
         h_planes1 = gain_out_of_psum(z_banks1, vector_banks=0)
+        h_grouped1 = regroup(nc.scalar.copy, h_planes1[:], "h_grouped")
         project(0, 2)
-        h_grouped1 = regroup(nc.vector.tensor_copy, h_planes1[:], "h_grouped")
         quantise(h_grouped1, s_codes[:, 1, :], s_scales[:, 1, :])
         for s in range(PARTS):
             project(1, s)

@@ -44,7 +44,7 @@ def tile_swintransformerblock_pa_kernel(
         keep = ctx.enter_context(tc.tile_pool(name="keep", bufs=1))
         small = ctx.enter_context(tc.tile_pool(name="small", bufs=2))
         z_pool = ctx.enter_context(tc.tile_pool(name="z_pool", bufs=4))
-        stage = ctx.enter_context(tc.tile_pool(name="stage", bufs=2))
+        stage = ctx.enter_context(tc.tile_pool(name="stage", bufs=3))
         t_psum = ctx.enter_context(tc.psum_pool(name="t_psum", bufs=1))
         acc_psum = ctx.enter_context(tc.psum_pool(name="acc_psum", bufs=4))
 
@@ -72,11 +72,11 @@ def tile_swintransformerblock_pa_kernel(
         load_w(0)
         load_x(2 * LOAD_LANES)
         load_x(3 * LOAD_LANES)
+        load_w(1)
+        load_w(2)
         nc.sync.dma_start(
             out=bias_all[:].rearrange("m s n -> m (s n)"), in_=qkv2_b.partition_broadcast(P)
         )
-        load_w(1)
-        load_w(2)
 
         eps = const.tile([P, 1], F32)
         nc.vector.memset(eps[:], EPS)
@@ -110,18 +110,23 @@ def tile_swintransformerblock_pa_kernel(
 
         gain_cols = const.tile([P, 2 * PACK], F32)
 
+        gain_rows_f32 = const.tile([P, P], F32)
+
         def gains_onto_partitions():
-            gain_rows_f32 = const.tile([P, P], F32)
-            nc.vector.tensor_copy(out=gain_rows_f32[:], in_=gain_rows[:])
             gain_bank = acc_psum.tile([P, P], F32, tag="acc")
             nc.tensor.transpose(out=gain_bank[:], in_=gain_rows_f32[:], identity=ident[:])
             nc.scalar.copy(out=gain_cols[:], in_=gain_bank[:, 0 : 2 * PACK])
 
-        def regroup(copy, planes, name):
+        def gpsimd_copy(out, in_):
+            nc.gpsimd.tensor_scalar(
+                out=out, in0=in_, scalar1=1.0, scalar2=0.0, op0=ALU.mult, op1=ALU.add
+            )
+
+        def regroup(copy, planes, name, run):
             grouped = stage.tile([P, D, PACK], BF16, align_bytes=64, name=name, tag=name)
             copy(
-                out=grouped[:].rearrange("p (c i) t -> p c t i", i=4),
-                in_=planes.rearrange("p t (c i) -> p c t i", i=4),
+                out=grouped[:].rearrange("p (c i) t -> p c t i", i=run),
+                in_=planes.rearrange("p t (c i) -> p c t i", i=run),
             )
             return grouped
 
@@ -164,23 +169,13 @@ def tile_swintransformerblock_pa_kernel(
             ]
             for u in range(ROW_LANES):
                 z = z_pool.tile([P, D], F32)
-                if u < ROW_LANES // 2:
-                    nc.scalar.activation(
-                        out=z[:],
-                        in_=x_sb[:, r * ROW_LANES + u, :],
-                        func=ACT.Identity,
-                        scale=rstd[:, u : u + 1],
-                        bias=shift[:, u : u + 1],
-                    )
-                else:
-                    nc.gpsimd.tensor_scalar(
-                        out=z[:],
-                        in0=x_sb[:, r * ROW_LANES + u, :],
-                        scalar1=rstd[:, u : u + 1],
-                        scalar2=shift[:, u : u + 1],
-                        op0=ALU.mult,
-                        op1=ALU.add,
-                    )
+                nc.scalar.activation(
+                    out=z[:],
+                    in_=x_sb[:, r * ROW_LANES + u, :],
+                    func=ACT.Identity,
+                    scale=rstd[:, u : u + 1],
+                    bias=shift[:, u : u + 1],
+                )
                 q = (u + 2) % ROW_LANES
                 permutation = take_below_right if u < 2 else take_below
                 for t in range(PACK):
@@ -252,26 +247,27 @@ def tile_swintransformerblock_pa_kernel(
                         ].rearrange("m n q c -> m n (q c)"),
                     )
 
-        rstd0, shift0 = row_scales(row_moments(0))
-        z_banks0 = normalise_and_transpose(0, rstd0, shift0)
+        w_grouped0 = regroup(gpsimd_copy, w_sb[:, 0, :, :], "w_grouped", run=1)
+        w_grouped1 = regroup(gpsimd_copy, w_sb[:, 1, :, :], "w_grouped", run=1)
+        mean_var0 = row_moments(0)
+        nc.vector.tensor_copy(out=gain_rows_f32[:], in_=gain_rows[:])
+        rstd0, shift0 = row_scales(mean_var0)
         gains_onto_partitions()
-        mean_var1 = row_moments(1)
-        w_grouped0 = regroup(nc.vector.tensor_copy, w_sb[:, 0, :, :], "w_grouped")
-        quantise(w_grouped0, w_codes[:, 0, :], w_scales[:, 0, :])
+        z_banks0 = normalise_and_transpose(0, rstd0, shift0)
+        rstd1, shift1 = row_scales(row_moments(1))
         h_planes0 = gain_out_of_psum(z_banks0, vector_banks=2)
-        h_grouped0 = regroup(nc.vector.tensor_copy, h_planes0[:], "h_grouped")
-        rstd1, shift1 = row_scales(mean_var1)
-        quantise(h_grouped0, s_codes[:, 0, :], s_scales[:, 0, :])
-        w_grouped1 = regroup(nc.scalar.copy, w_sb[:, 1, :, :], "w_grouped")
-        project(0, 0)
-        quantise(w_grouped1, w_codes[:, 1, :], w_scales[:, 1, :])
         z_banks1 = normalise_and_transpose(1, rstd1, shift1)
-        w_grouped2 = regroup(nc.scalar.copy, w_sb[:, 2, :, :], "w_grouped")
-        project(0, 1)
-        quantise(w_grouped2, w_codes[:, 2, :], w_scales[:, 2, :])
+        h_grouped0 = regroup(nc.vector.tensor_copy, h_planes0[:], "h_grouped", run=4)
+        quantise(w_grouped0, w_codes[:, 0, :], w_scales[:, 0, :])
+        quantise(w_grouped1, w_codes[:, 1, :], w_scales[:, 1, :])
+        quantise(h_grouped0, s_codes[:, 0, :], s_scales[:, 0, :])
+        w_grouped2 = regroup(nc.scalar.copy, w_sb[:, 2, :, :], "w_grouped", run=4)
         h_planes1 = gain_out_of_psum(z_banks1, vector_banks=0)
-        h_grouped1 = regroup(nc.scalar.copy, h_planes1[:], "h_grouped")
-        project(0, 2)
+        h_grouped1 = regroup(nc.scalar.copy, h_planes1[:], "h_grouped", run=4)
+        project(0, 0)
+        quantise(w_grouped2, w_codes[:, 2, :], w_scales[:, 2, :])
+        project(0, 1)
         quantise(h_grouped1, s_codes[:, 1, :], s_scales[:, 1, :])
+        project(0, 2)
         for s in range(PARTS):
             project(1, s)

@@ -117,16 +117,11 @@ def tile_swintransformerblock_pa_kernel(
             nc.tensor.transpose(out=gain_bank[:], in_=gain_rows_f32[:], identity=ident[:])
             nc.scalar.copy(out=gain_cols[:], in_=gain_bank[:, 0 : 2 * PACK])
 
-        def gpsimd_copy(out, in_):
-            nc.gpsimd.tensor_scalar(
-                out=out, in0=in_, scalar1=1.0, scalar2=0.0, op0=ALU.mult, op1=ALU.add
-            )
-
-        def regroup(copy, planes, name, run):
+        def regroup(copy, planes, name):
             grouped = stage.tile([P, D, PACK], BF16, align_bytes=64, name=name, tag=name)
             copy(
-                out=grouped[:].rearrange("p (c i) t -> p c t i", i=run),
-                in_=planes.rearrange("p t (c i) -> p c t i", i=run),
+                out=grouped[:].rearrange("p (c i) t -> p c t i", i=4),
+                in_=planes.rearrange("p t (c i) -> p c t i", i=4),
             )
             return grouped
 
@@ -169,13 +164,23 @@ def tile_swintransformerblock_pa_kernel(
             ]
             for u in range(ROW_LANES):
                 z = z_pool.tile([P, D], F32)
-                nc.scalar.activation(
-                    out=z[:],
-                    in_=x_sb[:, r * ROW_LANES + u, :],
-                    func=ACT.Identity,
-                    scale=rstd[:, u : u + 1],
-                    bias=shift[:, u : u + 1],
-                )
+                if u < ROW_LANES // 2:
+                    nc.scalar.activation(
+                        out=z[:],
+                        in_=x_sb[:, r * ROW_LANES + u, :],
+                        func=ACT.Identity,
+                        scale=rstd[:, u : u + 1],
+                        bias=shift[:, u : u + 1],
+                    )
+                else:
+                    nc.gpsimd.tensor_scalar(
+                        out=z[:],
+                        in0=x_sb[:, r * ROW_LANES + u, :],
+                        scalar1=rstd[:, u : u + 1],
+                        scalar2=shift[:, u : u + 1],
+                        op0=ALU.mult,
+                        op1=ALU.add,
+                    )
                 q = (u + 2) % ROW_LANES
                 permutation = take_below_right if u < 2 else take_below
                 for t in range(PACK):
@@ -247,8 +252,6 @@ def tile_swintransformerblock_pa_kernel(
                         ].rearrange("m n q c -> m n (q c)"),
                     )
 
-        w_grouped0 = regroup(gpsimd_copy, w_sb[:, 0, :, :], "w_grouped", run=1)
-        w_grouped1 = regroup(gpsimd_copy, w_sb[:, 1, :, :], "w_grouped", run=1)
         mean_var0 = row_moments(0)
         nc.vector.tensor_copy(out=gain_rows_f32[:], in_=gain_rows[:])
         rstd0, shift0 = row_scales(mean_var0)
@@ -257,13 +260,15 @@ def tile_swintransformerblock_pa_kernel(
         rstd1, shift1 = row_scales(row_moments(1))
         h_planes0 = gain_out_of_psum(z_banks0, vector_banks=2)
         z_banks1 = normalise_and_transpose(1, rstd1, shift1)
-        h_grouped0 = regroup(nc.vector.tensor_copy, h_planes0[:], "h_grouped", run=4)
+        w_grouped0 = regroup(nc.vector.tensor_copy, w_sb[:, 0, :, :], "w_grouped")
+        h_grouped0 = regroup(nc.vector.tensor_copy, h_planes0[:], "h_grouped")
         quantise(w_grouped0, w_codes[:, 0, :], w_scales[:, 0, :])
-        quantise(w_grouped1, w_codes[:, 1, :], w_scales[:, 1, :])
+        w_grouped1 = regroup(nc.scalar.copy, w_sb[:, 1, :, :], "w_grouped")
         quantise(h_grouped0, s_codes[:, 0, :], s_scales[:, 0, :])
-        w_grouped2 = regroup(nc.scalar.copy, w_sb[:, 2, :, :], "w_grouped", run=4)
+        quantise(w_grouped1, w_codes[:, 1, :], w_scales[:, 1, :])
+        w_grouped2 = regroup(nc.scalar.copy, w_sb[:, 2, :, :], "w_grouped")
         h_planes1 = gain_out_of_psum(z_banks1, vector_banks=0)
-        h_grouped1 = regroup(nc.scalar.copy, h_planes1[:], "h_grouped", run=4)
+        h_grouped1 = regroup(nc.scalar.copy, h_planes1[:], "h_grouped")
         project(0, 0)
         quantise(w_grouped2, w_codes[:, 2, :], w_scales[:, 2, :])
         project(0, 1)

from contextlib import ExitStack

import concourse.mybir as mybir
from concourse.masks import make_identity

F32 = mybir.dt.float32
BF16 = mybir.dt.bfloat16
I32 = mybir.dt.int32
U32 = mybir.dt.uint32
U8 = mybir.dt.uint8
FP8X4 = mybir.dt.float8_e4m3fn_x4
ACT = mybir.ActivationFunctionType
ALU = mybir.AluOpType

P = 128
PACK = 4
D = P * PACK
GRID = 8
WINDOWS = GRID * GRID
LANES = 8
ROW_LANES = 4
ROUNDS = LANES // ROW_LANES
PARTS = 3
HEADS = 8
HEAD_DIM = D // HEADS
PASS_HEADS = 4
PASS_COLS = PASS_HEADS * HEAD_DIM
BANK_LANES = 2
LOAD_LANES = 2
EPS = 1e-5

FLOPS = 2 * (P * LANES) * D * (PARTS * D)


def tile_swintransformerblock_pa_kernel(
    tc, x_win, ln3_g, ln3_b, qkv2_w, qkv2_b, out_0, out_1, out_2
):
    nc = tc.nc
    outs = (out_0, out_1, out_2)

    with ExitStack() as ctx:
        ctx.enter_context(tc.manual_schedule())
        const = ctx.enter_context(tc.tile_pool(name="const", bufs=1))
        keep = ctx.enter_context(tc.tile_pool(name="keep", bufs=1))
        small = ctx.enter_context(tc.tile_pool(name="small", bufs=2))
        z_pool = ctx.enter_context(tc.tile_pool(name="z_pool", bufs=4))
        stage = ctx.enter_context(tc.tile_pool(name="stage", bufs=3))
        t_psum = ctx.enter_context(tc.psum_pool(name="t_psum", bufs=1))
        acc_psum = ctx.enter_context(tc.psum_pool(name="acc_psum", bufs=4))

        x_sb = keep.tile([P, LANES, D], BF16)
        x_rows = x_win.rearrange("(i j) d -> i j d", j=LANES)
        w_sb = keep.tile([P, PARTS, PACK, D], BF16)
        w_rows = qkv2_w.rearrange("(t p) (s n) -> p s t n", p=P, s=PARTS)
        gain_rows = const.tile([P, P], BF16)
        nc.vector.memset(gain_rows[:].bitcast(I32), 0)
        bias_all = const.tile([P, PARTS, D], BF16)

        def load_x(lane0):
            lanes = slice(lane0, lane0 + LOAD_LANES)
            nc.sync.dma_start(out=x_sb[:, lanes, :], in_=x_rows[:, lanes, :])

        def load_w(s):
            nc.sync.dma_start(out=w_sb[:, s, :, :], in_=w_rows[:, s, :, :])

        load_x(0)
        load_x(LOAD_LANES)
        nc.sync.dma_start(out=gain_rows[0:PACK, :], in_=ln3_g.rearrange("(t p) -> t p", p=P))
        nc.sync.dma_start(
            out=gain_rows[PACK : 2 * PACK, :], in_=ln3_b.rearrange("(t p) -> t p", p=P)
        )
        load_w(0)
        load_x(2 * LOAD_LANES)
        load_x(3 * LOAD_LANES)
        load_w(1)
        load_w(2)
        nc.sync.dma_start(
            out=bias_all[:].rearrange("m s n -> m (s n)"), in_=qkv2_b.partition_broadcast(P)
        )

        eps = const.tile([P, 1], F32)
        nc.vector.memset(eps[:], EPS)
        table_warmer = const.tile([P, 1], F32)
        nc.scalar.activation(out=table_warmer[:], in_=eps[:], func=ACT.Sqrt)

        ident = const.tile([P, P], F32)
        make_identity(nc, ident[:])

        take_below = const.tile([P, P], F32)
        from_half = ident[:].rearrange("i (w h) -> i w h", h=2)
        to_half = take_below[:].rearrange("i (w h) -> i w h", h=2)
        nc.vector.tensor_copy(out=to_half[:, :, 0], in_=from_half[:, :, 1])
        nc.vector.tensor_copy(
            out=to_half[:, 0 : WINDOWS - GRID, 1], in_=from_half[:, GRID:WINDOWS, 0]
        )
        nc.vector.tensor_copy(
            out=to_half[:, WINDOWS - GRID : WINDOWS, 1], in_=from_half[:, 0:GRID, 0]
        )
        take_below_right = const.tile([P, P], F32)
        from_row = take_below[:].rearrange("i (r e) -> i r e", e=2 * GRID)
        to_row = take_below_right[:].rearrange("i (r e) -> i r e", e=2 * GRID)
        nc.vector.tensor_copy(out=to_row[:, :, 0 : 2 * GRID - 2], in_=from_row[:, :, 2 : 2 * GRID])
        nc.vector.tensor_copy(out=to_row[:, :, 2 * GRID - 2 : 2 * GRID], in_=from_row[:, :, 0:2])

        s_codes = keep.tile([P, ROUNDS, ROW_LANES * P], U32, align_bytes=64)
        s_scales = keep.tile([P, ROUNDS, ROW_LANES * P], U8, align_bytes=64)
        w_codes = keep.tile([P, PARTS, D], U32, align_bytes=64)
        w_scales = keep.tile([P, PARTS, D], U8, align_bytes=64)
        out_sb = keep.tile([P, PARTS, HEADS, LANES, HEAD_DIM], F32)

        gain_cols = const.tile([P, 2 * PACK], F32)

        gain_rows_f32 = const.tile([P, P], F32)

        def gains_onto_partitions():
            gain_bank = acc_psum.tile([P, P], F32, tag="acc")
            nc.tensor.transpose(out=gain_bank[:], in_=gain_rows_f32[:], identity=ident[:])
            nc.scalar.copy(out=gain_cols[:], in_=gain_bank[:, 0 : 2 * PACK])

        def regroup(copy, planes, name):
            grouped = stage.tile([P, D, PACK], BF16, align_bytes=64, name=name, tag=name)
            copy(
                out=grouped[:].rearrange("p (c i) t -> p c t i", i=4),
                in_=planes.rearrange("p t (c i) -> p c t i", i=4),
            )
            return grouped

        def quantise(grouped, codes, scales):
            nc.vector.quantize_mx(
                out=codes.bitcast(FP8X4),
                scales=scales,
                in_=grouped[:].rearrange("p c t -> p (c t)"),
            )

        def row_moments(r):
            stats = small.tile([P, ROW_LANES, 6], F32)
            mean_var = small.tile([P, ROW_LANES, 2], F32)
            for u in range(ROW_LANES):
                nc.vector.bn_stats(out=stats[:, u, :], in_=x_sb[:, r * ROW_LANES + u, :])
            for u in range(ROW_LANES):
                nc.vector.bn_aggr(out=mean_var[:, u, :], in_=stats[:, u, :])
            return mean_var

        def row_scales(mean_var):
            std = small.tile([P, ROW_LANES], F32)
            nc.scalar.activation(out=std[:], in_=mean_var[:, :, 1], func=ACT.Sqrt, bias=eps[:])
            rstd = small.tile([P, ROW_LANES], F32)
            nc.vector.reciprocal(out=rstd[:], in_=std[:])
            shift = small.tile([P, ROW_LANES], F32)
            nc.vector.scalar_tensor_tensor(
                out=shift[:],
                in0=mean_var[:, :, 0],
                scalar=-1.0,
                in1=rstd[:],
                op0=ALU.mult,
                op1=ALU.mult,
            )
            return rstd, shift

        def normalise_and_transpose(r, rstd, shift):
            z_banks = [
                t_psum.tile([P, ROW_LANES, P], F32, name="z_bank%d" % t, tag="z_bank%d" % t)
                for t in range(PACK)
            ]
            for u in range(ROW_LANES):
                z = z_pool.tile([P, D], F32)
                if u < ROW_LANES // 2:
                    nc.scalar.activation(
                        out=z[:],
                        in_=x_sb[:, r * ROW_LANES + u, :],
                        func=ACT.Identity,
                        scale=rstd[:, u : u + 1],
                        bias=shift[:, u : u + 1],
                    )
                else:
                    nc.gpsimd.tensor_scalar(
                        out=z[:],
                        in0=x_sb[:, r * ROW_LANES + u, :],
                        scalar1=rstd[:, u : u + 1],
                        scalar2=shift[:, u : u + 1],
                        op0=ALU.mult,
                        op1=ALU.add,
                    )
                q = (u + 2) % ROW_LANES
                permutation = take_below_right if u < 2 else take_below
                for t in range(PACK):
                    nc.tensor.transpose(
                        out=z_banks[t][:, q, :],
                        in_=z[:, t * P : (t + 1) * P],
                        identity=permutation[:],
                    )
            return z_banks

        def gain_out_of_psum(z_banks, vector_banks):
            h_planes = stage.tile([P, PACK, ROW_LANES * P], BF16)
            for t in range(PACK):
                z_bank = z_banks[t][:].rearrange("p q m -> p (q m)")
                gain = gain_cols[:, t : t + 1]
                bias = gain_cols[:, PACK + t : PACK + t + 1]
                if t < PACK - vector_banks:
                    nc.scalar.activation(
                        out=h_planes[:, t, :], in_=z_bank, func=ACT.Identity, scale=gain, bias=bias
                    )
                else:
                    nc.vector.tensor_scalar(
                        out=h_planes[:, t, :],
                        in0=z_bank,
                        scalar1=gain,
                        scalar2=bias,
                        op0=ALU.mult,
                        op1=ALU.add,
                    )
            return h_planes

        def project(r, s):
            dram = outs[s].rearrange("w n (h r q) c -> h r w n (q c)", h=2, r=ROUNDS)
            for n0 in range(0, HEADS, PASS_HEADS):
                cols = slice(n0 * HEAD_DIM, n0 * HEAD_DIM + PASS_COLS)
                for q0 in range(0, ROW_LANES, BANK_LANES):
                    acc = acc_psum.tile([P, BANK_LANES, PASS_COLS], F32, tag="acc")
                    for e in range(BANK_LANES):
                        rows = slice((q0 + e) * P, (q0 + e + 1) * P)
                        nc.tensor.matmul_mx(
                            out=acc[:, e, :],
                            lhsT=s_codes[:, r, rows].bitcast(FP8X4),
                            lhsT_scale=s_scales[:, r, rows],
                            rhs=w_codes[:, s, cols].bitcast(FP8X4),
                            rhs_scale=w_scales[:, s, cols],
                            start=True,
                            stop=True,
                        )
                    lane0 = r * ROW_LANES + q0
                    nc.vector.tensor_tensor(
                        out=out_sb[
                            :, s, n0 : n0 + PASS_HEADS, lane0 : lane0 + BANK_LANES, :
                        ].rearrange("m n q c -> m q n c"),
                        in0=acc[:].rearrange("m q (n c) -> m q n c", c=HEAD_DIM),
                        in1=bias_all[:, s, cols]
                        .rearrange("m (o n c) -> m o n c", o=1, c=HEAD_DIM)
                        .to_broadcast([P, BANK_LANES, PASS_HEADS, HEAD_DIM]),
                        op=ALU.add,
                    )
                for half in range(2):
                    nc.sync.dma_start(
                        out=dram[half, r, :, n0 : n0 + PASS_HEADS, :],
                        in_=out_sb[
                            half:P:2,
                            s,
                            n0 : n0 + PASS_HEADS,
                            r * ROW_LANES : (r + 1) * ROW_LANES,
                            :,
                        ].rearrange("m n q c -> m n (q c)"),
                    )

        mean_var0 = row_moments(0)
        nc.vector.tensor_copy(out=gain_rows_f32[:], in_=gain_rows[:])
        rstd0, shift0 = row_scales(mean_var0)
        gains_onto_partitions()
        z_banks0 = normalise_and_transpose(0, rstd0, shift0)
        rstd1, shift1 = row_scales(row_moments(1))
        h_planes0 = gain_out_of_psum(z_banks0, vector_banks=2)
        z_banks1 = normalise_and_transpose(1, rstd1, shift1)
        w_grouped0 = regroup(nc.vector.tensor_copy, w_sb[:, 0, :, :], "w_grouped")
        h_grouped0 = regroup(nc.vector.tensor_copy, h_planes0[:], "h_grouped")
        quantise(w_grouped0, w_codes[:, 0, :], w_scales[:, 0, :])
        w_grouped1 = regroup(nc.scalar.copy, w_sb[:, 1, :, :], "w_grouped")
        quantise(h_grouped0, s_codes[:, 0, :], s_scales[:, 0, :])
        quantise(w_grouped1, w_codes[:, 1, :], w_scales[:, 1, :])
        w_grouped2 = regroup(nc.scalar.copy, w_sb[:, 2, :, :], "w_grouped")
        h_planes1 = gain_out_of_psum(z_banks1, vector_banks=0)
        h_grouped1 = regroup(nc.scalar.copy, h_planes1[:], "h_grouped")
        project(0, 0)
        quantise(w_grouped2, w_codes[:, 2, :], w_scales[:, 2, :])
        project(0, 1)
        quantise(h_grouped1, s_codes[:, 1, :], s_scales[:, 1, :])
        project(0, 2)
        for s in range(PARTS):
            project(1, s)
